import numpy as np
import ml_dtypes

BF16 = ml_dtypes.bfloat16


def bf(x):
    return np.asarray(x, np.float32).astype(BF16)


def f32(x):
    return np.asarray(x, np.float32)


def f64(x):
    return np.asarray(x).astype(np.float64)


def striped(idx):
    return np.tile(idx.reshape(-1, 16).T, (8, 1))


C, S, H, K, N = 512, 512, 256, 4, 1024
EPS = 1e-8
LABEL_SMOOTH = 0.05


def setup_inputs():
    init = np.full((C, S), np.log((LABEL_SMOOTH + EPS) / (S - 1)))
    np.fill_diagonal(init, np.log(1.0 - LABEL_SMOOTH + EPS))
    cm = f32(init + np.random.standard_normal((C, S)))
    logits = f32(np.random.standard_normal((C, N)))
    idx = np.concatenate([np.random.permutation(S)[:H] for _ in range(K)])
    return {"cm": cm, "logits": logits, "offs": striped(idx)}


def reference(cm, logits, offs):
    idx = offs[:16].T.reshape(-1)
    m = f64(cm)
    lcm = m - np.log(np.exp(m).sum(axis=1, keepdims=True))
    return lcm[:, idx] + f64(logits)

@@ -1,0 +1,60 @@
+import concourse.mybir as mybir
+
+P = 128
+C, S, N = 512, 512, 1024
+BLOCKS = C // P
+PIECE = S
+PIECES = N // PIECE
+PIECE_COLUMNS = PIECE // 16
+
+F32 = mybir.dt.float32
+U16 = mybir.dt.uint16
+ACT = mybir.ActivationFunctionType
+ADD = mybir.AluOpType.add
+X = mybir.AxisListType.X
+
+
+def tile_emloss_kernel(tc, cm, logits, offs, out):
+    nc = tc.nc
+    with (
+        tc.tile_pool(name="held", bufs=1) as held,
+        tc.tile_pool(name="scratch", bufs=2) as scratch,
+    ):
+        offsets = held.tile([P, N // 16], U16, name="offsets")
+        nc.sync.dma_start(offsets[:], offs)
+
+        raw = []
+        for b in range(BLOCKS):
+            raw.append(held.tile([P, S], F32, name=f"raw{b}"))
+            nc.sync.dma_start(raw[b][:], cm[b * P : (b + 1) * P, :])
+        scores = {}
+        for b in range(BLOCKS):
+            for h in range(PIECES):
+                scores[b, h] = held.tile([P, PIECE], F32, name=f"scores{b}_{h}")
+                nc.sync.dma_start(
+                    scores[b, h][:], logits[b * P : (b + 1) * P, h * PIECE : (h + 1) * PIECE]
+                )
+
+        negmax = []
+        for b in range(BLOCKS):
+            negmax.append(held.tile([P, 1], F32, name=f"negmax{b}"))
+            nc.vector.reduce_max(negmax[b][:], raw[b][:], axis=X, negate=True)
+
+        lcm = []
+        for b in range(BLOCKS):
+            exped = scratch.tile([P, S], F32, name="exped")
+            total = held.tile([P, 1], F32, name=f"total{b}")
+            nc.scalar.activation(exped[:], raw[b][:], ACT.Exp, bias=negmax[b][:], accum_out=total[:])
+            logsum = held.tile([P, 1], F32, name=f"logsum{b}")
+            nc.scalar.activation(logsum[:], total[:], ACT.Ln)
+            shift = held.tile([P, 1], F32, name=f"shift{b}")
+            nc.scalar.activation(shift[:], logsum[:], ACT.Identity, bias=negmax[b][:], scale=-1.0)
+            lcm.append(held.tile([P, S], F32, name=f"lcm{b}"))
+            nc.scalar.activation(lcm[b][:], raw[b][:], ACT.Identity, bias=shift[:])
+
+        for b in range(BLOCKS):
+            for h in range(PIECES):
+                joint = held.tile([P, PIECE], F32, name=f"joint{b}_{h}")
+                picked = lcm[b][:].indirect(offsets[:, h * PIECE_COLUMNS : (h + 1) * PIECE_COLUMNS])
+                nc.vector.tensor_tensor(joint[:], picked, scores[b, h][:], ADD)
+                nc.sync.dma_start(out[b * P : (b + 1) * P, h * PIECE : (h + 1) * PIECE], joint[:])

@@ -10,7 +10,7 @@ PIECE_COLUMNS = PIECE // 16
 F32 = mybir.dt.float32
 U16 = mybir.dt.uint16
 ACT = mybir.ActivationFunctionType
-ADD = mybir.AluOpType.add
+ALU = mybir.AluOpType
 X = mybir.AxisListType.X
 
 
@@ -20,13 +20,17 @@ def tile_emloss_kernel(tc, cm, logits, offs, out):
         tc.tile_pool(name="held", bufs=1) as held,
         tc.tile_pool(name="scratch", bufs=2) as scratch,
     ):
-        offsets = held.tile([P, N // 16], U16, name="offsets")
-        nc.sync.dma_start(offsets[:], offs)
+
+        warm = held.tile([P, 1], F32, name="warm")
+        nc.vector.memset(warm[:], 0.0)
+        nc.scalar.activation(warm[:], warm[:], ACT.Exp)
 
         raw = []
         for b in range(BLOCKS):
             raw.append(held.tile([P, S], F32, name=f"raw{b}"))
             nc.sync.dma_start(raw[b][:], cm[b * P : (b + 1) * P, :])
+        offsets = held.tile([P, N // 16], U16, name="offsets")
+        nc.sync.dma_start(offsets[:], offs)
         scores = {}
         for b in range(BLOCKS):
             for h in range(PIECES):
@@ -35,26 +39,28 @@ def tile_emloss_kernel(tc, cm, logits, offs, out):
                     scores[b, h][:], logits[b * P : (b + 1) * P, h * PIECE : (h + 1) * PIECE]
                 )
 
-        negmax = []
-        for b in range(BLOCKS):
-            negmax.append(held.tile([P, 1], F32, name=f"negmax{b}"))
-            nc.vector.reduce_max(negmax[b][:], raw[b][:], axis=X, negate=True)
+        negmax = held.tile([P, BLOCKS], F32, name="negmax")
+        total = held.tile([P, BLOCKS], F32, name="total")
+        logsum = held.tile([P, BLOCKS], F32, name="logsum")
+        shift = held.tile([P, BLOCKS], F32, name="shift")
 
-        lcm = []
         for b in range(BLOCKS):
+            nc.vector.reduce_max(negmax[:, b : b + 1], raw[b][:], axis=X, negate=True)
             exped = scratch.tile([P, S], F32, name="exped")
-            total = held.tile([P, 1], F32, name=f"total{b}")
-            nc.scalar.activation(exped[:], raw[b][:], ACT.Exp, bias=negmax[b][:], accum_out=total[:])
-            logsum = held.tile([P, 1], F32, name=f"logsum{b}")
-            nc.scalar.activation(logsum[:], total[:], ACT.Ln)
-            shift = held.tile([P, 1], F32, name=f"shift{b}")
-            nc.scalar.activation(shift[:], logsum[:], ACT.Identity, bias=negmax[b][:], scale=-1.0)
-            lcm.append(held.tile([P, S], F32, name=f"lcm{b}"))
-            nc.scalar.activation(lcm[b][:], raw[b][:], ACT.Identity, bias=shift[:])
+            nc.scalar.activation(
+                exped[:], raw[b][:], ACT.Exp, bias=negmax[:, b : b + 1], accum_out=total[:, b : b + 1]
+            )
+        nc.scalar.activation(logsum[:], total[:], ACT.Ln)
+        nc.vector.tensor_tensor(shift[:], negmax[:], logsum[:], ALU.subtract)
+
+        lcm = [held.tile([P, S], F32, name=f"lcm{b}") for b in range(BLOCKS)]
+        nc.vector.tensor_scalar_add(lcm[0][:], raw[0][:], shift[:, 0:1])
+        for b in range(1, BLOCKS):
+            nc.scalar.activation(lcm[b][:], raw[b][:], ACT.Identity, bias=shift[:, b : b + 1])
 
         for b in range(BLOCKS):
             for h in range(PIECES):
                 joint = held.tile([P, PIECE], F32, name=f"joint{b}_{h}")
                 picked = lcm[b][:].indirect(offsets[:, h * PIECE_COLUMNS : (h + 1) * PIECE_COLUMNS])
-                nc.vector.tensor_tensor(joint[:], picked, scores[b, h][:], ADD)
+                nc.vector.tensor_tensor(joint[:], picked, scores[b, h][:], ALU.add)
                 nc.sync.dma_start(out[b * P : (b + 1) * P, h * PIECE : (h + 1) * PIECE], joint[:])

@@ -46,17 +46,28 @@ def tile_emloss_kernel(tc, cm, logits, offs, out):
 
         for b in range(BLOCKS):
             nc.vector.reduce_max(negmax[:, b : b + 1], raw[b][:], axis=X, negate=True)
-            exped = scratch.tile([P, S], F32, name="exped")
-            nc.scalar.activation(
-                exped[:], raw[b][:], ACT.Exp, bias=negmax[:, b : b + 1], accum_out=total[:, b : b + 1]
-            )
-        nc.scalar.activation(logsum[:], total[:], ACT.Ln)
-        nc.vector.tensor_tensor(shift[:], negmax[:], logsum[:], ALU.subtract)
 
         lcm = [held.tile([P, S], F32, name=f"lcm{b}") for b in range(BLOCKS)]
-        nc.vector.tensor_scalar_add(lcm[0][:], raw[0][:], shift[:, 0:1])
-        for b in range(1, BLOCKS):
-            nc.scalar.activation(lcm[b][:], raw[b][:], ACT.Identity, bias=shift[:, b : b + 1])
+        for group in (range(0, BLOCKS - 1), range(BLOCKS - 1, BLOCKS)):
+            for b in group:
+                exped = scratch.tile([P, S], F32, name="exped") if b < BLOCKS - 1 else raw[0]
+                nc.scalar.activation(
+                    exped[:], raw[b][:], ACT.Exp, bias=negmax[:, b : b + 1], accum_out=total[:, b : b + 1]
+                )
+            nc.scalar.activation(logsum[:, group[0] : group[-1] + 1], total[:, group[0] : group[-1] + 1], ACT.Ln)
+
+            for b in group:
+                if b == 0:
+                    nc.vector.tensor_scalar(
+                        lcm[b][:], raw[b][:], negmax[:, b : b + 1], logsum[:, b : b + 1],
+                        op0=ALU.add, op1=ALU.subtract,
+                    )
+                else:
+                    nc.scalar.activation(
+                        shift[:, b : b + 1], logsum[:, b : b + 1], ACT.Identity,
+                        bias=negmax[:, b : b + 1], scale=-1.0,
+                    )
+                    nc.scalar.activation(lcm[b][:], raw[b][:], ACT.Identity, bias=shift[:, b : b + 1])
 
         for b in range(BLOCKS):
             for h in range(PIECES):

@@ -4,8 +4,9 @@ P = 128
 C, S, N = 512, 512, 1024
 BLOCKS = C // P
 PIECE = S
-PIECES = N // PIECE
-PIECE_COLUMNS = PIECE // 16
+
+WHOLE_PIECES = [(j, j + PIECE) for j in range(0, N, PIECE)]
+PIECES = [WHOLE_PIECES] * (BLOCKS - 1) + [WHOLE_PIECES[:-1] + [(N - PIECE, N - PIECE // 2), (N - PIECE // 2, N)]]
 
 F32 = mybir.dt.float32
 U16 = mybir.dt.uint16
@@ -33,11 +34,9 @@ def tile_emloss_kernel(tc, cm, logits, offs, out):
         nc.sync.dma_start(offsets[:], offs)
         scores = {}
         for b in range(BLOCKS):
-            for h in range(PIECES):
-                scores[b, h] = held.tile([P, PIECE], F32, name=f"scores{b}_{h}")
-                nc.sync.dma_start(
-                    scores[b, h][:], logits[b * P : (b + 1) * P, h * PIECE : (h + 1) * PIECE]
-                )
+            for j, k in PIECES[b]:
+                scores[b, j] = held.tile([P, k - j], F32, name=f"scores{b}_{j}")
+                nc.sync.dma_start(scores[b, j][:], logits[b * P : (b + 1) * P, j:k])
 
         negmax = held.tile([P, BLOCKS], F32, name="negmax")
         total = held.tile([P, BLOCKS], F32, name="total")
@@ -70,8 +69,8 @@ def tile_emloss_kernel(tc, cm, logits, offs, out):
                     nc.scalar.activation(lcm[b][:], raw[b][:], ACT.Identity, bias=shift[:, b : b + 1])
 
         for b in range(BLOCKS):
-            for h in range(PIECES):
-                joint = held.tile([P, PIECE], F32, name=f"joint{b}_{h}")
-                picked = lcm[b][:].indirect(offsets[:, h * PIECE_COLUMNS : (h + 1) * PIECE_COLUMNS])
-                nc.vector.tensor_tensor(joint[:], picked, scores[b, h][:], ALU.add)
-                nc.sync.dma_start(out[b * P : (b + 1) * P, h * PIECE : (h + 1) * PIECE], joint[:])
+            for j, k in PIECES[b]:
+                joint = held.tile([P, k - j], F32, name=f"joint{b}_{j}")
+                picked = lcm[b][:].indirect(offsets[:, j // 16 : k // 16])
+                nc.vector.tensor_tensor(joint[:], picked, scores[b, j][:], ALU.add)
+                nc.sync.dma_start(out[b * P : (b + 1) * P, j:k], joint[:])

import concourse.mybir as mybir

P = 128
C, S, N = 512, 512, 1024
BLOCKS = C // P
PIECE = S

WHOLE_PIECES = [(j, j + PIECE) for j in range(0, N, PIECE)]
PIECES = [WHOLE_PIECES] * (BLOCKS - 1) + [WHOLE_PIECES[:-1] + [(N - PIECE, N - PIECE // 2), (N - PIECE // 2, N)]]

F32 = mybir.dt.float32
U16 = mybir.dt.uint16
ACT = mybir.ActivationFunctionType
ALU = mybir.AluOpType
X = mybir.AxisListType.X


def tile_emloss_kernel(tc, cm, logits, offs, out):
    nc = tc.nc
    with (
        tc.tile_pool(name="held", bufs=1) as held,
        tc.tile_pool(name="scratch", bufs=2) as scratch,
    ):

        warm = held.tile([P, 1], F32, name="warm")
        nc.vector.memset(warm[:], 0.0)
        nc.scalar.activation(warm[:], warm[:], ACT.Exp)

        raw = []
        for b in range(BLOCKS):
            raw.append(held.tile([P, S], F32, name=f"raw{b}"))
            nc.sync.dma_start(raw[b][:], cm[b * P : (b + 1) * P, :])
        offsets = held.tile([P, N // 16], U16, name="offsets")
        nc.sync.dma_start(offsets[:], offs)
        scores = {}
        for b in range(BLOCKS):
            for j, k in PIECES[b]:
                scores[b, j] = held.tile([P, k - j], F32, name=f"scores{b}_{j}")
                nc.sync.dma_start(scores[b, j][:], logits[b * P : (b + 1) * P, j:k])

        negmax = held.tile([P, BLOCKS], F32, name="negmax")
        total = held.tile([P, BLOCKS], F32, name="total")
        logsum = held.tile([P, BLOCKS], F32, name="logsum")
        shift = held.tile([P, BLOCKS], F32, name="shift")

        for b in range(BLOCKS):
            nc.vector.reduce_max(negmax[:, b : b + 1], raw[b][:], axis=X, negate=True)

        lcm = [held.tile([P, S], F32, name=f"lcm{b}") for b in range(BLOCKS)]
        for group in (range(0, BLOCKS - 1), range(BLOCKS - 1, BLOCKS)):
            for b in group:
                exped = scratch.tile([P, S], F32, name="exped") if b < BLOCKS - 1 else raw[0]
                nc.scalar.activation(
                    exped[:], raw[b][:], ACT.Exp, bias=negmax[:, b : b + 1], accum_out=total[:, b : b + 1]
                )
            nc.scalar.activation(logsum[:, group[0] : group[-1] + 1], total[:, group[0] : group[-1] + 1], ACT.Ln)

            for b in group:
                if b == 0:
                    nc.vector.tensor_scalar(
                        lcm[b][:], raw[b][:], negmax[:, b : b + 1], logsum[:, b : b + 1],
                        op0=ALU.add, op1=ALU.subtract,
                    )
                else:
                    nc.scalar.activation(
                        shift[:, b : b + 1], logsum[:, b : b + 1], ACT.Identity,
                        bias=negmax[:, b : b + 1], scale=-1.0,
                    )
                    nc.scalar.activation(lcm[b][:], raw[b][:], ACT.Identity, bias=shift[:, b : b + 1])

        for b in range(BLOCKS):
            for j, k in PIECES[b]:
                joint = held.tile([P, k - j], F32, name=f"joint{b}_{j}")
                picked = lcm[b][:].indirect(offsets[:, j // 16 : k // 16])
                nc.vector.tensor_tensor(joint[:], picked, scores[b, j][:], ALU.add)
                nc.sync.dma_start(out[b * P : (b + 1) * P, j:k], joint[:])
